import numpy as np
import ml_dtypes

BF16 = ml_dtypes.bfloat16


def bf(x):
    return np.asarray(x, np.float32).astype(BF16)


def f32(x):
    return np.asarray(x, np.float32)


def f64(x):
    return np.asarray(x).astype(np.float64)


def striped(idx):
    return np.tile(idx.reshape(-1, 16).T, (8, 1))


CF, CP, Q, S, N = 256, 128, 4, 256, 512


def sigmoid(v):
    return 1.0 / (1.0 + np.exp(-v))


def setup_inputs():
    return {"scene": f32(0.25 * np.random.standard_normal((Q * CP, S))), "proposal": bf(np.random.standard_normal((CF, N))), "w_prop": bf(np.random.standard_normal((CF, CP)) / np.sqrt(CF)), "b_prop": f32(0.3 * np.random.standard_normal((CP, 1))), "w_fc": f32(0.25 * np.random.standard_normal((1, Q))), "b_fc": f32(0.5 + 0.1 * np.random.standard_normal((1,))), "offs": striped(np.random.permutation(np.tile(np.arange(S), 2))[:N])}


def reference(scene, proposal, w_prop, b_prop, w_fc, b_fc, offs):
    idx = offs[:16].T.reshape(-1)
    p = f64(w_prop).T @ f64(proposal) + f64(b_prop)
    prod = f64(scene)[:, idx].reshape(Q, CP, N) * p[None, :, :]
    logit = np.einsum("q,qn->n", f64(w_fc)[0], prod.sum(axis=1)) + f64(b_fc)[0]
    a = sigmoid(logit)
    return f64(proposal) * (1.0 + a[None, :])

@@ -1,0 +1,73 @@
+import concourse.mybir as mybir
+
+F32 = mybir.dt.float32
+BF16 = mybir.dt.bfloat16
+U16 = mybir.dt.uint16
+MULT = mybir.AluOpType.mult
+ADD = mybir.AluOpType.add
+FUNC = mybir.ActivationFunctionType
+
+P = 128
+CF, CP, Q, S, N = 256, 128, 4, 256, 512
+KB = CF // P
+PIECE = 256
+PIECES = N // PIECE
+FLOPS = 2 * CF * CP * N + 2 * Q * CP * N
+
+
+def tile_contextawareattention_kernel(tc, scene, proposal, w_prop, b_prop, w_fc, b_fc, offs, out):
+    nc = tc.nc
+    with (
+        tc.tile_pool(name="held", bufs=1) as held,
+        tc.tile_pool(name="work", bufs=4) as work,
+        tc.psum_pool(name="psum", bufs=2) as psum,
+    ):
+        offsets = held.tile([P, N // 16], U16, name="offsets")
+        nc.sync.dma_start(offsets[:], offs)
+
+        weights = [held.tile([P, CP], BF16, name=f"weights{k}") for k in range(KB)]
+        features = [held.tile([P, N], BF16, name=f"features{k}") for k in range(KB)]
+        for k in range(KB):
+            nc.scalar.dma_start(weights[k][:], w_prop[k * P : (k + 1) * P, :])
+            nc.sync.dma_start(features[k][:], proposal[k * P : (k + 1) * P, :])
+
+        windows = [held.tile([P, S], F32, name=f"window{q}") for q in range(Q)]
+        for q in range(Q):
+            nc.scalar.dma_start(windows[q][:], scene[q * P : (q + 1) * P, :])
+
+        bias_p = held.tile([P, 1], F32, name="bias_p")
+        fc_w = held.tile([P, Q], F32, name="fc_w")
+        fc_b = held.tile([P, 1], F32, name="fc_b")
+        with nc.allow_non_contiguous_dma(reason="three small vectors, one or four elements to a partition"):
+            nc.gpsimd.dma_start(bias_p[:], b_prop)
+            nc.gpsimd.dma_start(fc_w[:], w_fc.broadcast_to([P, Q]))
+            nc.gpsimd.dma_start(fc_b[:], b_fc.partition_broadcast(P))
+
+        ones = held.tile([P, P], BF16, name="ones")
+        nc.vector.memset(ones[:], 1.0)
+
+        for i in range(PIECES):
+            cols = slice(i * PIECE, (i + 1) * PIECE)
+
+            p_psum = psum.tile([P, PIECE], F32, name="p_psum")
+            for k in range(KB):
+                nc.tensor.matmul(p_psum[:], weights[k][:], features[k][:, cols], start=(k == 0), stop=(k == KB - 1))
+            p = work.tile([P, PIECE], F32, name="p")
+            nc.scalar.activation(p[:], p_psum[:], FUNC.Identity, bias=bias_p[:])
+
+            logit = psum.tile([P, PIECE], F32, name="logit")
+            for q in range(Q):
+                picked = windows[q][:].indirect(offsets[:, i * (PIECE // 16) : (i + 1) * (PIECE // 16)])
+                match = work.tile([P, PIECE], F32, name="match")
+                nc.vector.tensor_tensor(match[:], picked, p[:], MULT)
+                weighted = work.tile([P, PIECE], BF16, name="weighted")
+                nc.scalar.activation(weighted[:], match[:], FUNC.Copy, scale=fc_w[:, q : q + 1])
+                nc.tensor.matmul(logit[:], ones[:], weighted[:], start=(q == 0), stop=(q == Q - 1))
+
+            gate = work.tile([P, PIECE], F32, name="gate")
+            nc.scalar.activation(gate[:], logit[:], FUNC.Sigmoid, bias=fc_b[:])
+
+            for k in range(KB):
+                gated = work.tile([P, PIECE], F32, name="gated")
+                nc.vector.scalar_tensor_tensor(gated[:], gate[:], 1.0, features[k][:, cols], ADD, MULT)
+                nc.sync.dma_start(out[k * P : (k + 1) * P, cols], gated[:])

@@ -20,54 +20,64 @@ def tile_contextawareattention_kernel(tc, scene, proposal, w_prop, b_prop, w_fc,
     with (
         tc.tile_pool(name="held", bufs=1) as held,
         tc.tile_pool(name="work", bufs=4) as work,
-        tc.psum_pool(name="psum", bufs=2) as psum,
+        tc.psum_pool(name="psum", bufs=1) as psum,
     ):
         offsets = held.tile([P, N // 16], U16, name="offsets")
         nc.sync.dma_start(offsets[:], offs)
 
-        weights = [held.tile([P, CP], BF16, name=f"weights{k}") for k in range(KB)]
-        features = [held.tile([P, N], BF16, name=f"features{k}") for k in range(KB)]
-        for k in range(KB):
-            nc.scalar.dma_start(weights[k][:], w_prop[k * P : (k + 1) * P, :])
-            nc.sync.dma_start(features[k][:], proposal[k * P : (k + 1) * P, :])
-
-        windows = [held.tile([P, S], F32, name=f"window{q}") for q in range(Q)]
-        for q in range(Q):
-            nc.scalar.dma_start(windows[q][:], scene[q * P : (q + 1) * P, :])
+        weights = held.tile([P, KB, CP], BF16, name="weights")
+        nc.scalar.dma_start(weights[:], w_prop.rearrange("(k r) c -> r k c", r=P))
+        features = held.tile([P, KB, N], BF16, name="features")
+        nc.sync.dma_start(features[:], proposal.rearrange("(k r) n -> r k n", r=P))
+        out_blocks = out.rearrange("(k r) n -> r k n", r=P)
 
         bias_p = held.tile([P, 1], F32, name="bias_p")
         fc_w = held.tile([P, Q], F32, name="fc_w")
         fc_b = held.tile([P, 1], F32, name="fc_b")
         with nc.allow_non_contiguous_dma(reason="three small vectors, one or four elements to a partition"):
-            nc.gpsimd.dma_start(bias_p[:], b_prop)
-            nc.gpsimd.dma_start(fc_w[:], w_fc.broadcast_to([P, Q]))
-            nc.gpsimd.dma_start(fc_b[:], b_fc.partition_broadcast(P))
+            nc.scalar.dma_start(bias_p[:], b_prop)
+            nc.scalar.dma_start(fc_w[:], w_fc.broadcast_to([P, Q]))
+            nc.scalar.dma_start(fc_b[:], b_fc.partition_broadcast(P))
+
+        windows = [held.tile([P, S], F32, name=f"window{q}") for q in range(Q)]
+        for q in range(Q):
+            queue = nc.sync if q % 2 == 0 else nc.scalar
+            queue.dma_start(windows[q][:], scene[q * P : (q + 1) * P, :])
 
         ones = held.tile([P, P], BF16, name="ones")
         nc.vector.memset(ones[:], 1.0)
 
+        warm = held.tile([P, 1], F32, name="warm")
+        nc.vector.memset(warm[:], 0.0)
+        nc.scalar.activation(warm[:], warm[:], FUNC.Sigmoid)
+
+        p_psum = psum.tile([P, N], F32, name="p_psum")
+        for k in range(KB):
+            nc.tensor.matmul(p_psum[:], weights[:, k, :], features[:, k, :], start=(k == 0), stop=(k == KB - 1))
+        p = held.tile([P, N], F32, name="p")
         for i in range(PIECES):
             cols = slice(i * PIECE, (i + 1) * PIECE)
+            nc.scalar.activation(p[:, cols], p_psum[:, cols], FUNC.Identity, bias=bias_p[:])
 
-            p_psum = psum.tile([P, PIECE], F32, name="p_psum")
-            for k in range(KB):
-                nc.tensor.matmul(p_psum[:], weights[k][:], features[k][:, cols], start=(k == 0), stop=(k == KB - 1))
-            p = work.tile([P, PIECE], F32, name="p")
-            nc.scalar.activation(p[:], p_psum[:], FUNC.Identity, bias=bias_p[:])
-
-            logit = psum.tile([P, PIECE], F32, name="logit")
-            for q in range(Q):
-                picked = windows[q][:].indirect(offsets[:, i * (PIECE // 16) : (i + 1) * (PIECE // 16)])
-                match = work.tile([P, PIECE], F32, name="match")
-                nc.vector.tensor_tensor(match[:], picked, p[:], MULT)
-                weighted = work.tile([P, PIECE], BF16, name="weighted")
-                nc.scalar.activation(weighted[:], match[:], FUNC.Copy, scale=fc_w[:, q : q + 1])
-                nc.tensor.matmul(logit[:], ones[:], weighted[:], start=(q == 0), stop=(q == Q - 1))
-
-            gate = work.tile([P, PIECE], F32, name="gate")
-            nc.scalar.activation(gate[:], logit[:], FUNC.Sigmoid, bias=fc_b[:])
-
-            for k in range(KB):
-                gated = work.tile([P, PIECE], F32, name="gated")
-                nc.vector.scalar_tensor_tensor(gated[:], gate[:], 1.0, features[k][:, cols], ADD, MULT)
-                nc.sync.dma_start(out[k * P : (k + 1) * P, cols], gated[:])
+        gates = []
+        for i in range(PIECES + 1):
+            if i < PIECES:
+                cols = slice(i * PIECE, (i + 1) * PIECE)
+                logit = psum.tile([P, PIECE], F32, name=f"logit{i}")
+                for q in range(Q):
+                    picked = windows[q][:].indirect(offsets[:, i * (PIECE // 16) : (i + 1) * (PIECE // 16)])
+                    match = work.tile([P, PIECE], F32, name="match")
+                    nc.vector.tensor_tensor(match[:], picked, p[:, cols], MULT)
+                    weighted = work.tile([P, PIECE], BF16, name="weighted")
+                    nc.scalar.activation(weighted[:], match[:], FUNC.Copy, scale=fc_w[:, q : q + 1])
+                    nc.tensor.matmul(logit[:], ones[:], weighted[:], start=(q == 0), stop=(q == Q - 1))
+                gate = work.tile([P, PIECE], F32, name="gate")
+                nc.scalar.activation(gate[:], logit[:], FUNC.Sigmoid, bias=fc_b[:])
+                gates.append(gate)
+            if i >= 1:
+                cols = slice((i - 1) * PIECE, i * PIECE)
+                gated = work.tile([P, KB, PIECE], F32, name="gated")
+                nc.vector.scalar_tensor_tensor(
+                    gated[:], gates[i - 1][:].unsqueeze(1).to_broadcast([P, KB, PIECE]), 1.0, features[:, :, cols], ADD, MULT
+                )
+                nc.sync.dma_start(out_blocks[:, :, cols], gated[:])

@@ -10,7 +10,7 @@ FUNC = mybir.ActivationFunctionType
 P = 128
 CF, CP, Q, S, N = 256, 128, 4, 256, 512
 KB = CF // P
-PIECE = 256
+PIECE = 128
 PIECES = N // PIECE
 FLOPS = 2 * CF * CP * N + 2 * Q * CP * N
 
@@ -20,29 +20,27 @@ def tile_contextawareattention_kernel(tc, scene, proposal, w_prop, b_prop, w_fc,
     with (
         tc.tile_pool(name="held", bufs=1) as held,
         tc.tile_pool(name="work", bufs=4) as work,
-        tc.psum_pool(name="psum", bufs=1) as psum,
+        tc.psum_pool(name="psum", bufs=2) as psum,
     ):
-        offsets = held.tile([P, N // 16], U16, name="offsets")
-        nc.sync.dma_start(offsets[:], offs)
-
-        weights = held.tile([P, KB, CP], BF16, name="weights")
-        nc.scalar.dma_start(weights[:], w_prop.rearrange("(k r) c -> r k c", r=P))
         features = held.tile([P, KB, N], BF16, name="features")
-        nc.sync.dma_start(features[:], proposal.rearrange("(k r) n -> r k n", r=P))
-        out_blocks = out.rearrange("(k r) n -> r k n", r=P)
-
+        weights = held.tile([P, KB, CP], BF16, name="weights")
+        offsets = held.tile([P, N // 16], U16, name="offsets")
         bias_p = held.tile([P, 1], F32, name="bias_p")
         fc_w = held.tile([P, Q], F32, name="fc_w")
         fc_b = held.tile([P, 1], F32, name="fc_b")
-        with nc.allow_non_contiguous_dma(reason="three small vectors, one or four elements to a partition"):
+        windows = [held.tile([P, S], F32, name=f"window{q}") for q in range(Q)]
+
+        nc.sync.dma_start(features[:, 0, :], proposal[0:P, :])
+        nc.scalar.dma_start(weights[:], w_prop.rearrange("(k r) c -> r k c", r=P))
+        nc.scalar.dma_start(features[:, 1, :], proposal[P : 2 * P, :])
+        nc.sync.dma_start(offsets[:], offs)
+        with nc.allow_non_contiguous_dma(reason="small vectors, one or four elements to a partition"):
             nc.scalar.dma_start(bias_p[:], b_prop)
             nc.scalar.dma_start(fc_w[:], w_fc.broadcast_to([P, Q]))
-            nc.scalar.dma_start(fc_b[:], b_fc.partition_broadcast(P))
-
-        windows = [held.tile([P, S], F32, name=f"window{q}") for q in range(Q)]
         for q in range(Q):
-            queue = nc.sync if q % 2 == 0 else nc.scalar
-            queue.dma_start(windows[q][:], scene[q * P : (q + 1) * P, :])
+            nc.sync.dma_start(windows[q][:], scene[q * P : (q + 1) * P, :])
+        with nc.allow_non_contiguous_dma(reason="one element to a partition"):
+            nc.sync.dma_start(fc_b[:], b_fc.partition_broadcast(P))
 
         ones = held.tile([P, P], BF16, name="ones")
         nc.vector.memset(ones[:], 1.0)
@@ -51,33 +49,32 @@ def tile_contextawareattention_kernel(tc, scene, proposal, w_prop, b_prop, w_fc,
         nc.vector.memset(warm[:], 0.0)
         nc.scalar.activation(warm[:], warm[:], FUNC.Sigmoid)
 
-        p_psum = psum.tile([P, N], F32, name="p_psum")
-        for k in range(KB):
-            nc.tensor.matmul(p_psum[:], weights[:, k, :], features[:, k, :], start=(k == 0), stop=(k == KB - 1))
         p = held.tile([P, N], F32, name="p")
         for i in range(PIECES):
             cols = slice(i * PIECE, (i + 1) * PIECE)
-            nc.scalar.activation(p[:, cols], p_psum[:, cols], FUNC.Identity, bias=bias_p[:])
+            p_psum = psum.tile([P, PIECE], F32, name="p_psum")
+            for k in range(KB):
+                nc.tensor.matmul(p_psum[:], weights[:, k, :], features[:, k, cols], start=(k == 0), stop=(k == KB - 1))
+            nc.scalar.activation(p[:, cols], p_psum[:], FUNC.Identity, bias=bias_p[:])
 
-        gates = []
-        for i in range(PIECES + 1):
-            if i < PIECES:
-                cols = slice(i * PIECE, (i + 1) * PIECE)
-                logit = psum.tile([P, PIECE], F32, name=f"logit{i}")
-                for q in range(Q):
-                    picked = windows[q][:].indirect(offsets[:, i * (PIECE // 16) : (i + 1) * (PIECE // 16)])
-                    match = work.tile([P, PIECE], F32, name="match")
-                    nc.vector.tensor_tensor(match[:], picked, p[:, cols], MULT)
-                    weighted = work.tile([P, PIECE], BF16, name="weighted")
-                    nc.scalar.activation(weighted[:], match[:], FUNC.Copy, scale=fc_w[:, q : q + 1])
-                    nc.tensor.matmul(logit[:], ones[:], weighted[:], start=(q == 0), stop=(q == Q - 1))
-                gate = work.tile([P, PIECE], F32, name="gate")
-                nc.scalar.activation(gate[:], logit[:], FUNC.Sigmoid, bias=fc_b[:])
-                gates.append(gate)
-            if i >= 1:
-                cols = slice((i - 1) * PIECE, i * PIECE)
-                gated = work.tile([P, KB, PIECE], F32, name="gated")
-                nc.vector.scalar_tensor_tensor(
-                    gated[:], gates[i - 1][:].unsqueeze(1).to_broadcast([P, KB, PIECE]), 1.0, features[:, :, cols], ADD, MULT
-                )
-                nc.sync.dma_start(out_blocks[:, :, cols], gated[:])
+        gate = held.tile([P, N], F32, name="gate")
+        for i in range(PIECES):
+            cols = slice(i * PIECE, (i + 1) * PIECE)
+            logit = psum.tile([P, PIECE], F32, name="logit")
+            for q in range(Q):
+                picked = windows[q][:].indirect(offsets[:, i * (PIECE // 16) : (i + 1) * (PIECE // 16)])
+                match = work.tile([P, PIECE], F32, name="match")
+                nc.vector.tensor_tensor(match[:], picked, p[:, cols], MULT)
+                weighted = work.tile([P, PIECE], BF16, name="weighted")
+                nc.scalar.activation(weighted[:], match[:], FUNC.Copy, scale=fc_w[:, q : q + 1])
+                nc.tensor.matmul(logit[:], ones[:], weighted[:], start=(q == 0), stop=(q == Q - 1))
+            nc.scalar.activation(gate[:, cols], logit[:], FUNC.Sigmoid, bias=fc_b[:])
+
+        out_blocks = out.rearrange("(k r) n -> r k n", r=P)
+        for i in range(PIECES):
+            cols = slice(i * PIECE, (i + 1) * PIECE)
+            gated = work.tile([P, KB, PIECE], F32, name="gated")
+            nc.vector.scalar_tensor_tensor(
+                gated[:], gate[:, cols].unsqueeze(1).to_broadcast([P, KB, PIECE]), 1.0, features[:, :, cols], ADD, MULT
+            )
+            nc.sync.dma_start(out_blocks[:, :, cols], gated[:])

@@ -10,18 +10,22 @@ FUNC = mybir.ActivationFunctionType
 P = 128
 CF, CP, Q, S, N = 256, 128, 4, 256, 512
 KB = CF // P
-PIECE = 128
-PIECES = N // PIECE
 FLOPS = 2 * CF * CP * N + 2 * Q * CP * N
+
+WIDTHS = (128, 256, 64, 64)
+assert sum(WIDTHS) == N and all(width % 32 == 0 and width <= S for width in WIDTHS)
+PIECES = [(sum(WIDTHS[:i]), WIDTHS[i]) for i in range(len(WIDTHS))]
 
 
 def tile_contextawareattention_kernel(tc, scene, proposal, w_prop, b_prop, w_fc, b_fc, offs, out):
     nc = tc.nc
     with (
         tc.tile_pool(name="held", bufs=1) as held,
-        tc.tile_pool(name="work", bufs=4) as work,
+        tc.tile_pool(name="work", bufs=8) as work,
         tc.psum_pool(name="psum", bufs=2) as psum,
     ):
+        proposal_blocks = proposal.rearrange("(k r) n -> r k n", r=P)
+        out_blocks = out.rearrange("(k r) n -> r k n", r=P)
         features = held.tile([P, KB, N], BF16, name="features")
         weights = held.tile([P, KB, CP], BF16, name="weights")
         offsets = held.tile([P, N // 16], U16, name="offsets")
@@ -30,16 +34,16 @@ def tile_contextawareattention_kernel(tc, scene, proposal, w_prop, b_prop, w_fc,
         fc_b = held.tile([P, 1], F32, name="fc_b")
         windows = [held.tile([P, S], F32, name=f"window{q}") for q in range(Q)]
 
-        nc.sync.dma_start(features[:, 0, :], proposal[0:P, :])
-        nc.scalar.dma_start(weights[:], w_prop.rearrange("(k r) c -> r k c", r=P))
-        nc.scalar.dma_start(features[:, 1, :], proposal[P : 2 * P, :])
-        nc.sync.dma_start(offsets[:], offs)
+        half = N // 2
         with nc.allow_non_contiguous_dma(reason="small vectors, one or four elements to a partition"):
             nc.scalar.dma_start(bias_p[:], b_prop)
+            nc.sync.dma_start(features[:, :, :half], proposal_blocks[:, :, :half])
+            nc.scalar.dma_start(weights[:], w_prop.rearrange("(k r) c -> r k c", r=P))
+            nc.sync.dma_start(offsets[:], offs)
+            nc.scalar.dma_start(features[:, :, half:], proposal_blocks[:, :, half:])
             nc.scalar.dma_start(fc_w[:], w_fc.broadcast_to([P, Q]))
-        for q in range(Q):
-            nc.sync.dma_start(windows[q][:], scene[q * P : (q + 1) * P, :])
-        with nc.allow_non_contiguous_dma(reason="one element to a partition"):
+            for q in range(Q):
+                nc.sync.dma_start(windows[q][:], scene[q * P : (q + 1) * P, :])
             nc.sync.dma_start(fc_b[:], b_fc.partition_broadcast(P))
 
         ones = held.tile([P, P], BF16, name="ones")
@@ -50,31 +54,30 @@ def tile_contextawareattention_kernel(tc, scene, proposal, w_prop, b_prop, w_fc,
         nc.scalar.activation(warm[:], warm[:], FUNC.Sigmoid)
 
         p = held.tile([P, N], F32, name="p")
-        for i in range(PIECES):
-            cols = slice(i * PIECE, (i + 1) * PIECE)
-            p_psum = psum.tile([P, PIECE], F32, name="p_psum")
+        for first, width in PIECES:
+            cols = slice(first, first + width)
+            p_psum = psum.tile([P, width], F32, name="p_psum")
             for k in range(KB):
                 nc.tensor.matmul(p_psum[:], weights[:, k, :], features[:, k, cols], start=(k == 0), stop=(k == KB - 1))
             nc.scalar.activation(p[:, cols], p_psum[:], FUNC.Identity, bias=bias_p[:])
 
         gate = held.tile([P, N], F32, name="gate")
-        for i in range(PIECES):
-            cols = slice(i * PIECE, (i + 1) * PIECE)
-            logit = psum.tile([P, PIECE], F32, name="logit")
+        for first, width in PIECES:
+            cols = slice(first, first + width)
+            logit = psum.tile([P, width], F32, name="logit")
             for q in range(Q):
-                picked = windows[q][:].indirect(offsets[:, i * (PIECE // 16) : (i + 1) * (PIECE // 16)])
-                match = work.tile([P, PIECE], F32, name="match")
+                picked = windows[q][:].indirect(offsets[:, first // 16 : (first + width) // 16])
+                match = work.tile([P, width], F32, name="match")
                 nc.vector.tensor_tensor(match[:], picked, p[:, cols], MULT)
-                weighted = work.tile([P, PIECE], BF16, name="weighted")
+                weighted = work.tile([P, width], BF16, name="weighted")
                 nc.scalar.activation(weighted[:], match[:], FUNC.Copy, scale=fc_w[:, q : q + 1])
                 nc.tensor.matmul(logit[:], ones[:], weighted[:], start=(q == 0), stop=(q == Q - 1))
             nc.scalar.activation(gate[:, cols], logit[:], FUNC.Sigmoid, bias=fc_b[:])
 
-        out_blocks = out.rearrange("(k r) n -> r k n", r=P)
-        for i in range(PIECES):
-            cols = slice(i * PIECE, (i + 1) * PIECE)
-            gated = work.tile([P, KB, PIECE], F32, name="gated")
+        for first, width in PIECES:
+            cols = slice(first, first + width)
+            gated = work.tile([P, KB, width], F32, name="gated")
             nc.vector.scalar_tensor_tensor(
-                gated[:], gate[:, cols].unsqueeze(1).to_broadcast([P, KB, PIECE]), 1.0, features[:, :, cols], ADD, MULT
+                gated[:], gate[:, cols].unsqueeze(1).to_broadcast([P, KB, width]), 1.0, features[:, :, cols], ADD, MULT
             )
             nc.sync.dma_start(out_blocks[:, :, cols], gated[:])

@@ -10,11 +10,9 @@ FUNC = mybir.ActivationFunctionType
 P = 128
 CF, CP, Q, S, N = 256, 128, 4, 256, 512
 KB = CF // P
+PIECE = 128
+PIECES = N // PIECE
 FLOPS = 2 * CF * CP * N + 2 * Q * CP * N
-
-WIDTHS = (128, 256, 64, 64)
-assert sum(WIDTHS) == N and all(width % 32 == 0 and width <= S for width in WIDTHS)
-PIECES = [(sum(WIDTHS[:i]), WIDTHS[i]) for i in range(len(WIDTHS))]
 
 
 def tile_contextawareattention_kernel(tc, scene, proposal, w_prop, b_prop, w_fc, b_fc, offs, out):
@@ -24,8 +22,6 @@ def tile_contextawareattention_kernel(tc, scene, proposal, w_prop, b_prop, w_fc,
         tc.tile_pool(name="work", bufs=8) as work,
         tc.psum_pool(name="psum", bufs=2) as psum,
     ):
-        proposal_blocks = proposal.rearrange("(k r) n -> r k n", r=P)
-        out_blocks = out.rearrange("(k r) n -> r k n", r=P)
         features = held.tile([P, KB, N], BF16, name="features")
         weights = held.tile([P, KB, CP], BF16, name="weights")
         offsets = held.tile([P, N // 16], U16, name="offsets")
@@ -34,50 +30,50 @@ def tile_contextawareattention_kernel(tc, scene, proposal, w_prop, b_prop, w_fc,
         fc_b = held.tile([P, 1], F32, name="fc_b")
         windows = [held.tile([P, S], F32, name=f"window{q}") for q in range(Q)]
 
-        half = N // 2
         with nc.allow_non_contiguous_dma(reason="small vectors, one or four elements to a partition"):
-            nc.scalar.dma_start(bias_p[:], b_prop)
-            nc.sync.dma_start(features[:, :, :half], proposal_blocks[:, :, :half])
+            nc.sync.dma_start(features[:], proposal.rearrange("(k r) n -> r k n", r=P))
             nc.scalar.dma_start(weights[:], w_prop.rearrange("(k r) c -> r k c", r=P))
             nc.sync.dma_start(offsets[:], offs)
-            nc.scalar.dma_start(features[:, :, half:], proposal_blocks[:, :, half:])
-            nc.scalar.dma_start(fc_w[:], w_fc.broadcast_to([P, Q]))
+            nc.scalar.dma_start(bias_p[:], b_prop)
             for q in range(Q):
-                nc.sync.dma_start(windows[q][:], scene[q * P : (q + 1) * P, :])
-            nc.sync.dma_start(fc_b[:], b_fc.partition_broadcast(P))
-
-        ones = held.tile([P, P], BF16, name="ones")
-        nc.vector.memset(ones[:], 1.0)
+                queue = nc.sync if q % 2 == 0 else nc.scalar
+                queue.dma_start(windows[q][:], scene[q * P : (q + 1) * P, :])
+            nc.gpsimd.dma_start(fc_w[:], w_fc.broadcast_to([P, Q]))
+            nc.gpsimd.dma_start(fc_b[:], b_fc.partition_broadcast(P))
 
         warm = held.tile([P, 1], F32, name="warm")
         nc.vector.memset(warm[:], 0.0)
         nc.scalar.activation(warm[:], warm[:], FUNC.Sigmoid)
 
+        ones = held.tile([P, P], BF16, name="ones")
+        nc.vector.memset(ones[:], 1.0)
+
         p = held.tile([P, N], F32, name="p")
-        for first, width in PIECES:
-            cols = slice(first, first + width)
-            p_psum = psum.tile([P, width], F32, name="p_psum")
+        for i in range(PIECES):
+            cols = slice(i * PIECE, (i + 1) * PIECE)
+            p_psum = psum.tile([P, PIECE], F32, name="p_psum")
             for k in range(KB):
                 nc.tensor.matmul(p_psum[:], weights[:, k, :], features[:, k, cols], start=(k == 0), stop=(k == KB - 1))
             nc.scalar.activation(p[:, cols], p_psum[:], FUNC.Identity, bias=bias_p[:])
 
         gate = held.tile([P, N], F32, name="gate")
-        for first, width in PIECES:
-            cols = slice(first, first + width)
-            logit = psum.tile([P, width], F32, name="logit")
+        for i in range(PIECES):
+            cols = slice(i * PIECE, (i + 1) * PIECE)
+            logit = psum.tile([P, PIECE], F32, name="logit")
             for q in range(Q):
-                picked = windows[q][:].indirect(offsets[:, first // 16 : (first + width) // 16])
-                match = work.tile([P, width], F32, name="match")
+                picked = windows[q][:].indirect(offsets[:, i * (PIECE // 16) : (i + 1) * (PIECE // 16)])
+                match = work.tile([P, PIECE], F32, name="match")
                 nc.vector.tensor_tensor(match[:], picked, p[:, cols], MULT)
-                weighted = work.tile([P, width], BF16, name="weighted")
+                weighted = work.tile([P, PIECE], BF16, name="weighted")
                 nc.scalar.activation(weighted[:], match[:], FUNC.Copy, scale=fc_w[:, q : q + 1])
                 nc.tensor.matmul(logit[:], ones[:], weighted[:], start=(q == 0), stop=(q == Q - 1))
             nc.scalar.activation(gate[:, cols], logit[:], FUNC.Sigmoid, bias=fc_b[:])
 
-        for first, width in PIECES:
-            cols = slice(first, first + width)
-            gated = work.tile([P, KB, width], F32, name="gated")
+        out_blocks = out.rearrange("(k r) n -> r k n", r=P)
+        for i in range(PIECES):
+            cols = slice(i * PIECE, (i + 1) * PIECE)
+            gated = work.tile([P, KB, PIECE], F32, name="gated")
             nc.vector.scalar_tensor_tensor(
-                gated[:], gate[:, cols].unsqueeze(1).to_broadcast([P, KB, width]), 1.0, features[:, :, cols], ADD, MULT
+                gated[:], gate[:, cols].unsqueeze(1).to_broadcast([P, KB, PIECE]), 1.0, features[:, :, cols], ADD, MULT
             )
             nc.sync.dma_start(out_blocks[:, :, cols], gated[:])

@@ -21,6 +21,7 @@ def tile_contextawareattention_kernel(tc, scene, proposal, w_prop, b_prop, w_fc,
         tc.tile_pool(name="held", bufs=1) as held,
         tc.tile_pool(name="work", bufs=8) as work,
         tc.psum_pool(name="psum", bufs=2) as psum,
+        tc.psum_pool(name="sums", bufs=1) as sums,
     ):
         features = held.tile([P, KB, N], BF16, name="features")
         weights = held.tile([P, KB, CP], BF16, name="weights")
@@ -30,16 +31,19 @@ def tile_contextawareattention_kernel(tc, scene, proposal, w_prop, b_prop, w_fc,
         fc_b = held.tile([P, 1], F32, name="fc_b")
         windows = [held.tile([P, S], F32, name=f"window{q}") for q in range(Q)]
 
+        proposal_blocks = proposal.rearrange("(k r) n -> r k n", r=P)
         with nc.allow_non_contiguous_dma(reason="small vectors, one or four elements to a partition"):
-            nc.sync.dma_start(features[:], proposal.rearrange("(k r) n -> r k n", r=P))
+            nc.sync.dma_start(features[:, :, :PIECE], proposal_blocks[:, :, :PIECE])
             nc.scalar.dma_start(weights[:], w_prop.rearrange("(k r) c -> r k c", r=P))
+            nc.gpsimd.dma_start(windows[Q - 1][:], scene[(Q - 1) * P :, :])
             nc.sync.dma_start(offsets[:], offs)
             nc.scalar.dma_start(bias_p[:], b_prop)
-            for q in range(Q):
-                queue = nc.sync if q % 2 == 0 else nc.scalar
-                queue.dma_start(windows[q][:], scene[q * P : (q + 1) * P, :])
-            nc.gpsimd.dma_start(fc_w[:], w_fc.broadcast_to([P, Q]))
-            nc.gpsimd.dma_start(fc_b[:], b_fc.partition_broadcast(P))
+            nc.sync.dma_start(windows[0][:], scene[0:P, :])
+            nc.scalar.dma_start(windows[1][:], scene[P : 2 * P, :])
+            nc.sync.dma_start(features[:, :, PIECE:], proposal_blocks[:, :, PIECE:])
+            nc.scalar.dma_start(windows[2][:], scene[2 * P : 3 * P, :])
+            nc.sync.dma_start(fc_w[:], w_fc.broadcast_to([P, Q]))
+            nc.sync.dma_start(fc_b[:], b_fc.partition_broadcast(P))
 
         warm = held.tile([P, 1], F32, name="warm")
         nc.vector.memset(warm[:], 0.0)
@@ -57,9 +61,10 @@ def tile_contextawareattention_kernel(tc, scene, proposal, w_prop, b_prop, w_fc,
             nc.scalar.activation(p[:, cols], p_psum[:], FUNC.Identity, bias=bias_p[:])
 
         gate = held.tile([P, N], F32, name="gate")
+        logits = [sums.tile([P, PIECE], F32, name=f"logit{i}") for i in range(PIECES)]
         for i in range(PIECES):
             cols = slice(i * PIECE, (i + 1) * PIECE)
-            logit = psum.tile([P, PIECE], F32, name="logit")
+            logit = logits[i]
             for q in range(Q):
                 picked = windows[q][:].indirect(offsets[:, i * (PIECE // 16) : (i + 1) * (PIECE // 16)])
                 match = work.tile([P, PIECE], F32, name="match")
@@ -67,7 +72,9 @@ def tile_contextawareattention_kernel(tc, scene, proposal, w_prop, b_prop, w_fc,
                 weighted = work.tile([P, PIECE], BF16, name="weighted")
                 nc.scalar.activation(weighted[:], match[:], FUNC.Copy, scale=fc_w[:, q : q + 1])
                 nc.tensor.matmul(logit[:], ones[:], weighted[:], start=(q == 0), stop=(q == Q - 1))
-            nc.scalar.activation(gate[:, cols], logit[:], FUNC.Sigmoid, bias=fc_b[:])
+            if i >= 1:
+                nc.scalar.activation(gate[:, (i - 1) * PIECE : i * PIECE], logits[i - 1][:], FUNC.Sigmoid, bias=fc_b[:])
+        nc.scalar.activation(gate[:, N - PIECE :], logits[PIECES - 1][:], FUNC.Sigmoid, bias=fc_b[:])
 
         out_blocks = out.rearrange("(k r) n -> r k n", r=P)
         for i in range(PIECES):

@@ -31,17 +31,14 @@ def tile_contextawareattention_kernel(tc, scene, proposal, w_prop, b_prop, w_fc,
         fc_b = held.tile([P, 1], F32, name="fc_b")
         windows = [held.tile([P, S], F32, name=f"window{q}") for q in range(Q)]
 
-        proposal_blocks = proposal.rearrange("(k r) n -> r k n", r=P)
         with nc.allow_non_contiguous_dma(reason="small vectors, one or four elements to a partition"):
-            nc.sync.dma_start(features[:, :, :PIECE], proposal_blocks[:, :, :PIECE])
-            nc.scalar.dma_start(weights[:], w_prop.rearrange("(k r) c -> r k c", r=P))
-            nc.gpsimd.dma_start(windows[Q - 1][:], scene[(Q - 1) * P :, :])
             nc.sync.dma_start(offsets[:], offs)
+            nc.scalar.dma_start(features[:], proposal.rearrange("(k r) n -> r k n", r=P))
+            nc.sync.dma_start(weights[:], w_prop.rearrange("(k r) c -> r k c", r=P))
             nc.scalar.dma_start(bias_p[:], b_prop)
-            nc.sync.dma_start(windows[0][:], scene[0:P, :])
-            nc.scalar.dma_start(windows[1][:], scene[P : 2 * P, :])
-            nc.sync.dma_start(features[:, :, PIECE:], proposal_blocks[:, :, PIECE:])
-            nc.scalar.dma_start(windows[2][:], scene[2 * P : 3 * P, :])
+            for q in range(Q):
+                queue = nc.sync if q % 2 == 0 else nc.scalar
+                queue.dma_start(windows[q][:], scene[q * P : (q + 1) * P, :])
             nc.sync.dma_start(fc_w[:], w_fc.broadcast_to([P, Q]))
             nc.sync.dma_start(fc_b[:], b_fc.partition_broadcast(P))
 

@@ -12,6 +12,7 @@ CF, CP, Q, S, N = 256, 128, 4, 256, 512
 KB = CF // P
 PIECE = 128
 PIECES = N // PIECE
+HALF = N // 2
 FLOPS = 2 * CF * CP * N + 2 * Q * CP * N
 
 
@@ -31,14 +32,16 @@ def tile_contextawareattention_kernel(tc, scene, proposal, w_prop, b_prop, w_fc,
         fc_b = held.tile([P, 1], F32, name="fc_b")
         windows = [held.tile([P, S], F32, name=f"window{q}") for q in range(Q)]
 
+        proposal_blocks = proposal.rearrange("(k r) n -> r k n", r=P)
         with nc.allow_non_contiguous_dma(reason="small vectors, one or four elements to a partition"):
             nc.sync.dma_start(offsets[:], offs)
-            nc.scalar.dma_start(features[:], proposal.rearrange("(k r) n -> r k n", r=P))
+            nc.scalar.dma_start(features[:, :, :HALF], proposal_blocks[:, :, :HALF])
             nc.sync.dma_start(weights[:], w_prop.rearrange("(k r) c -> r k c", r=P))
             nc.scalar.dma_start(bias_p[:], b_prop)
             for q in range(Q):
                 queue = nc.sync if q % 2 == 0 else nc.scalar
                 queue.dma_start(windows[q][:], scene[q * P : (q + 1) * P, :])
+            nc.sync.dma_start(features[:, :, HALF:], proposal_blocks[:, :, HALF:])
             nc.sync.dma_start(fc_w[:], w_fc.broadcast_to([P, Q]))
             nc.sync.dma_start(fc_b[:], b_fc.partition_broadcast(P))
 

@@ -10,8 +10,10 @@ FUNC = mybir.ActivationFunctionType
 P = 128
 CF, CP, Q, S, N = 256, 128, 4, 256, 512
 KB = CF // P
-PIECE = 128
-PIECES = N // PIECE
+WIDTHS = (64, 192, 192, 64)
+PIECES = len(WIDTHS)
+STARTS = [sum(WIDTHS[:i]) for i in range(PIECES)]
+assert sum(WIDTHS) == N
 HALF = N // 2
 FLOPS = 2 * CF * CP * N + 2 * Q * CP * N
 
@@ -54,33 +56,33 @@ def tile_contextawareattention_kernel(tc, scene, proposal, w_prop, b_prop, w_fc,
 
         p = held.tile([P, N], F32, name="p")
         for i in range(PIECES):
-            cols = slice(i * PIECE, (i + 1) * PIECE)
-            p_psum = psum.tile([P, PIECE], F32, name="p_psum")
+            cols = slice(STARTS[i], STARTS[i] + WIDTHS[i])
+            p_psum = psum.tile([P, WIDTHS[i]], F32, name="p_psum")
             for k in range(KB):
                 nc.tensor.matmul(p_psum[:], weights[:, k, :], features[:, k, cols], start=(k == 0), stop=(k == KB - 1))
             nc.scalar.activation(p[:, cols], p_psum[:], FUNC.Identity, bias=bias_p[:])
 
         gate = held.tile([P, N], F32, name="gate")
-        logits = [sums.tile([P, PIECE], F32, name=f"logit{i}") for i in range(PIECES)]
+        logits = [sums.tile([P, WIDTHS[i]], F32, name=f"logit{i}") for i in range(PIECES)]
         for i in range(PIECES):
-            cols = slice(i * PIECE, (i + 1) * PIECE)
+            cols = slice(STARTS[i], STARTS[i] + WIDTHS[i])
             logit = logits[i]
             for q in range(Q):
-                picked = windows[q][:].indirect(offsets[:, i * (PIECE // 16) : (i + 1) * (PIECE // 16)])
-                match = work.tile([P, PIECE], F32, name="match")
+                picked = windows[q][:].indirect(offsets[:, STARTS[i] // 16 : (STARTS[i] + WIDTHS[i]) // 16])
+                match = work.tile([P, WIDTHS[i]], F32, name="match")
                 nc.vector.tensor_tensor(match[:], picked, p[:, cols], MULT)
-                weighted = work.tile([P, PIECE], BF16, name="weighted")
+                weighted = work.tile([P, WIDTHS[i]], BF16, name="weighted")
                 nc.scalar.activation(weighted[:], match[:], FUNC.Copy, scale=fc_w[:, q : q + 1])
                 nc.tensor.matmul(logit[:], ones[:], weighted[:], start=(q == 0), stop=(q == Q - 1))
             if i >= 1:
-                nc.scalar.activation(gate[:, (i - 1) * PIECE : i * PIECE], logits[i - 1][:], FUNC.Sigmoid, bias=fc_b[:])
-        nc.scalar.activation(gate[:, N - PIECE :], logits[PIECES - 1][:], FUNC.Sigmoid, bias=fc_b[:])
+                nc.scalar.activation(gate[:, STARTS[i - 1] : STARTS[i]], logits[i - 1][:], FUNC.Sigmoid, bias=fc_b[:])
+        nc.scalar.activation(gate[:, STARTS[PIECES - 1] :], logits[PIECES - 1][:], FUNC.Sigmoid, bias=fc_b[:])
 
         out_blocks = out.rearrange("(k r) n -> r k n", r=P)
         for i in range(PIECES):
-            cols = slice(i * PIECE, (i + 1) * PIECE)
-            gated = work.tile([P, KB, PIECE], F32, name="gated")
+            cols = slice(STARTS[i], STARTS[i] + WIDTHS[i])
+            gated = work.tile([P, KB, WIDTHS[i]], F32, name="gated")
             nc.vector.scalar_tensor_tensor(
-                gated[:], gate[:, cols].unsqueeze(1).to_broadcast([P, KB, PIECE]), 1.0, features[:, :, cols], ADD, MULT
+                gated[:], gate[:, cols].unsqueeze(1).to_broadcast([P, KB, WIDTHS[i]]), 1.0, features[:, :, cols], ADD, MULT
             )
             nc.sync.dma_start(out_blocks[:, :, cols], gated[:])

@@ -85,4 +85,5 @@ def tile_contextawareattention_kernel(tc, scene, proposal, w_prop, b_prop, w_fc,
             nc.vector.scalar_tensor_tensor(
                 gated[:], gate[:, cols].unsqueeze(1).to_broadcast([P, KB, WIDTHS[i]]), 1.0, features[:, :, cols], ADD, MULT
             )
-            nc.sync.dma_start(out_blocks[:, :, cols], gated[:])
+            queue = nc.scalar if i == PIECES - 1 else nc.sync
+            queue.dma_start(out_blocks[:, :, cols], gated[:])

@@ -41,8 +41,7 @@ def tile_contextawareattention_kernel(tc, scene, proposal, w_prop, b_prop, w_fc,
             nc.sync.dma_start(weights[:], w_prop.rearrange("(k r) c -> r k c", r=P))
             nc.scalar.dma_start(bias_p[:], b_prop)
             for q in range(Q):
-                queue = nc.sync if q % 2 == 0 else nc.scalar
-                queue.dma_start(windows[q][:], scene[q * P : (q + 1) * P, :])
+                nc.sync.dma_start(windows[q][:], scene[q * P : (q + 1) * P, :])
             nc.sync.dma_start(features[:, :, HALF:], proposal_blocks[:, :, HALF:])
             nc.sync.dma_start(fc_w[:], w_fc.broadcast_to([P, Q]))
             nc.sync.dma_start(fc_b[:], b_fc.partition_broadcast(P))

import concourse.mybir as mybir

F32 = mybir.dt.float32
BF16 = mybir.dt.bfloat16
U16 = mybir.dt.uint16
MULT = mybir.AluOpType.mult
ADD = mybir.AluOpType.add
FUNC = mybir.ActivationFunctionType

P = 128
CF, CP, Q, S, N = 256, 128, 4, 256, 512
KB = CF // P
WIDTHS = (64, 192, 192, 64)
PIECES = len(WIDTHS)
STARTS = [sum(WIDTHS[:i]) for i in range(PIECES)]
assert sum(WIDTHS) == N
HALF = N // 2
FLOPS = 2 * CF * CP * N + 2 * Q * CP * N


def tile_contextawareattention_kernel(tc, scene, proposal, w_prop, b_prop, w_fc, b_fc, offs, out):
    nc = tc.nc
    with (
        tc.tile_pool(name="held", bufs=1) as held,
        tc.tile_pool(name="work", bufs=8) as work,
        tc.psum_pool(name="psum", bufs=2) as psum,
        tc.psum_pool(name="sums", bufs=1) as sums,
    ):
        features = held.tile([P, KB, N], BF16, name="features")
        weights = held.tile([P, KB, CP], BF16, name="weights")
        offsets = held.tile([P, N // 16], U16, name="offsets")
        bias_p = held.tile([P, 1], F32, name="bias_p")
        fc_w = held.tile([P, Q], F32, name="fc_w")
        fc_b = held.tile([P, 1], F32, name="fc_b")
        windows = [held.tile([P, S], F32, name=f"window{q}") for q in range(Q)]

        proposal_blocks = proposal.rearrange("(k r) n -> r k n", r=P)
        with nc.allow_non_contiguous_dma(reason="small vectors, one or four elements to a partition"):
            nc.sync.dma_start(offsets[:], offs)
            nc.scalar.dma_start(features[:, :, :HALF], proposal_blocks[:, :, :HALF])
            nc.sync.dma_start(weights[:], w_prop.rearrange("(k r) c -> r k c", r=P))
            nc.scalar.dma_start(bias_p[:], b_prop)
            for q in range(Q):
                nc.sync.dma_start(windows[q][:], scene[q * P : (q + 1) * P, :])
            nc.sync.dma_start(features[:, :, HALF:], proposal_blocks[:, :, HALF:])
            nc.sync.dma_start(fc_w[:], w_fc.broadcast_to([P, Q]))
            nc.sync.dma_start(fc_b[:], b_fc.partition_broadcast(P))

        warm = held.tile([P, 1], F32, name="warm")
        nc.vector.memset(warm[:], 0.0)
        nc.scalar.activation(warm[:], warm[:], FUNC.Sigmoid)

        ones = held.tile([P, P], BF16, name="ones")
        nc.vector.memset(ones[:], 1.0)

        p = held.tile([P, N], F32, name="p")
        for i in range(PIECES):
            cols = slice(STARTS[i], STARTS[i] + WIDTHS[i])
            p_psum = psum.tile([P, WIDTHS[i]], F32, name="p_psum")
            for k in range(KB):
                nc.tensor.matmul(p_psum[:], weights[:, k, :], features[:, k, cols], start=(k == 0), stop=(k == KB - 1))
            nc.scalar.activation(p[:, cols], p_psum[:], FUNC.Identity, bias=bias_p[:])

        gate = held.tile([P, N], F32, name="gate")
        logits = [sums.tile([P, WIDTHS[i]], F32, name=f"logit{i}") for i in range(PIECES)]
        for i in range(PIECES):
            cols = slice(STARTS[i], STARTS[i] + WIDTHS[i])
            logit = logits[i]
            for q in range(Q):
                picked = windows[q][:].indirect(offsets[:, STARTS[i] // 16 : (STARTS[i] + WIDTHS[i]) // 16])
                match = work.tile([P, WIDTHS[i]], F32, name="match")
                nc.vector.tensor_tensor(match[:], picked, p[:, cols], MULT)
                weighted = work.tile([P, WIDTHS[i]], BF16, name="weighted")
                nc.scalar.activation(weighted[:], match[:], FUNC.Copy, scale=fc_w[:, q : q + 1])
                nc.tensor.matmul(logit[:], ones[:], weighted[:], start=(q == 0), stop=(q == Q - 1))
            if i >= 1:
                nc.scalar.activation(gate[:, STARTS[i - 1] : STARTS[i]], logits[i - 1][:], FUNC.Sigmoid, bias=fc_b[:])
        nc.scalar.activation(gate[:, STARTS[PIECES - 1] :], logits[PIECES - 1][:], FUNC.Sigmoid, bias=fc_b[:])

        out_blocks = out.rearrange("(k r) n -> r k n", r=P)
        for i in range(PIECES):
            cols = slice(STARTS[i], STARTS[i] + WIDTHS[i])
            gated = work.tile([P, KB, WIDTHS[i]], F32, name="gated")
            nc.vector.scalar_tensor_tensor(
                gated[:], gate[:, cols].unsqueeze(1).to_broadcast([P, KB, WIDTHS[i]]), 1.0, features[:, :, cols], ADD, MULT
            )
            queue = nc.scalar if i == PIECES - 1 else nc.sync
            queue.dma_start(out_blocks[:, :, cols], gated[:])
